import numpy as np
import ml_dtypes


def mxq(x, axis, fmt="e4m3"):
    dtype, down = {"e4m3": (ml_dtypes.float8_e4m3fn, 7), "e5m2": (ml_dtypes.float8_e5m2, 14)}[fmt]
    v = np.moveaxis(np.asarray(x, np.float32).astype(ml_dtypes.bfloat16).astype(np.float64), axis, -1)
    blocks = v.reshape(v.shape[:-1] + (-1, 32))
    amax = np.abs(blocks).max(-1, keepdims=True)
    byte = np.maximum(np.where(amax > 0, np.frexp(amax)[1] - 1 + 127, 0) - down, 1)
    scale = np.exp2(byte - 127.0)
    codes = (blocks / scale).astype(np.float32).astype(dtype).astype(np.float64)
    return np.moveaxis((codes * scale).reshape(v.shape), -1, axis)


WIDE = False


def mx_kscale(k):
    if not WIDE:
        return np.ones(k)
    levels = np.array([10, -10, 5, -5, 0])
    if k % 512:
        return np.exp2(np.random.permutation(np.resize(levels, k // 32))).repeat(32)
    a = np.empty((k // 512, 16))
    for p in range(k // 512):
        a[p, :8] = np.random.permutation(np.resize(levels, 8))
        for g in range(8):
            far = levels[np.abs(levels - a[p, g]) >= 10]
            a[p, g + 8] = far[np.random.randint(len(far))]
    return np.exp2(a.ravel()).repeat(32)


BF16 = ml_dtypes.bfloat16


def bf(x):
    return np.asarray(x, np.float32).astype(BF16)


def f64(x):
    return np.asarray(x).astype(np.float64)


B, T, D, H = 4, 256, 512, 2048
N = B * T
EMA0 = 1.0


def sigmoid(v):
    return 1.0 / (1.0 + np.exp(-v))


def surprise_gate(err):
    err_mag = np.sqrt(np.sum(err * err)) / N
    ema = 0.95 * EMA0 + 0.05 * err_mag
    return np.minimum(err_mag / np.maximum(ema, 1e-8), 3.0)


def setup_inputs():
    s, t = mx_kscale(D), mx_kscale(N)
    return {"err": bf(np.random.standard_normal((N, D)) * 2.3 * s[None, :] * t[:, None]),
            "W_down": bf(np.random.standard_normal((D, H)) / np.sqrt(D) / s[:, None]),
            "gate_pre": bf(np.random.standard_normal((N, H))),
            "up_pre": bf(np.random.standard_normal((N, H))),
            "x_pred": bf(np.random.standard_normal((N, D)) / t[:, None])}


def reference(err, W_down, gate_pre, up_pre, x_pred):
    err, gate_pre, up_pre = f64(err), f64(gate_pre), f64(up_pre)
    sg = surprise_gate(err)
    d_h = mxq(err, 1, "e4m3") @ mxq(f64(W_down), 0, "e4m3")
    sig = sigmoid(gate_pre)
    gate_act = gate_pre * sig
    d_gate_act = d_h * up_pre
    d_up_val = d_h * gate_act
    d_gate_pre = d_gate_act * sig * (1.0 + gate_pre * (1.0 - sig))
    xq = mxq(f64(x_pred), 0, "e4m3")
    grad_gate = (mxq(d_gate_pre, 0, "e4m3").T @ xq) / N
    grad_up = (mxq(d_up_val, 0, "e4m3").T @ xq) / N
    return grad_up * sg, grad_gate * sg

@@ -1,0 +1,298 @@
+from contextlib import ExitStack
+
+import concourse.mybir as mybir
+from concourse.masks import make_identity
+
+F32 = mybir.dt.float32
+BF16 = mybir.dt.bfloat16
+U32 = mybir.dt.uint32
+U8 = mybir.dt.uint8
+FP8X4 = mybir.dt.float8_e4m3fn_x4
+ACT = mybir.ActivationFunctionType
+ALU = mybir.AluOpType
+
+N_TOK, D, H = 1024, 512, 2048
+FLOPS = 3 * 2 * N_TOK * D * H
+
+P = 128
+PACK = 4
+K_PASS = P * PACK
+G = N_TOK // K_PASS
+HT = 128
+N_HT = H // HT
+HB = 256
+N_HB = H // HB
+HL = 512
+N_HL = H // HL
+BANK_DT = F32
+
+
+def tile_continuummemorysystem_pa_kernel(tc, err, W_down, gate_pre, up_pre, x_pred, out_0, out_1):
+    nc = tc.nc
+    outs = (out_0, out_1)
+
+    with ExitStack() as ctx:
+        keep = ctx.enter_context(tc.tile_pool(name="keep", bufs=1))
+        raw = ctx.enter_context(tc.tile_pool(name="raw", bufs=4))
+        grp = ctx.enter_context(tc.tile_pool(name="grp", bufs=3))
+        elem = ctx.enter_context(tc.tile_pool(name="elem", bufs=2))
+        prod = ctx.enter_context(tc.tile_pool(name="prod", bufs=3))
+        stage = ctx.enter_context(tc.tile_pool(name="stage", bufs=4))
+        psum = ctx.enter_context(tc.psum_pool(name="psum", bufs=4))
+
+        gate_sb = [keep.tile([P, G * PACK, HL], BF16, name="gate%d" % c, tag="gate%d" % c) for c in range(N_HL)]
+        up_sb = [keep.tile([P, G * PACK, HL], BF16, name="up%d" % c, tag="up%d" % c) for c in range(N_HL)]
+        w_codes = keep.tile([P, H], U32, name="w_codes", tag="w_codes", align_bytes=64)
+        w_scales = keep.tile([P, H], U8, name="w_scales", tag="w_scales", align_bytes=64)
+        e_codes = keep.tile([P, N_TOK], U32, name="e_codes", tag="e_codes", align_bytes=64)
+        e_scales = keep.tile([P, N_TOK], U8, name="e_scales", tag="e_scales", align_bytes=64)
+        x_codes = keep.tile([P, G * D], U32, name="x_codes", tag="x_codes", align_bytes=64)
+        x_scales = keep.tile([P, G * D], U8, name="x_scales", tag="x_scales", align_bytes=64)
+        ident = keep.tile([P, P], F32, name="ident", tag="ident")
+        ones = keep.tile([P, P], F32, name="ones", tag="ones")
+        diag = keep.tile([P, P], F32, name="diag", tag="diag")
+        ssq = keep.tile([P, 2], F32, name="ssq", tag="ssq")
+        warm_in = keep.tile([P, 1], F32, name="warm_in", tag="warm_in")
+        warm_out = keep.tile([P, 1], F32, name="warm_out", tag="warm_out")
+        em = keep.tile([P, 1], F32, name="em", tag="em")
+        ema = keep.tile([P, 1], F32, name="ema", tag="ema")
+        emc = keep.tile([P, 1], F32, name="emc", tag="emc")
+        rec = keep.tile([P, 1], F32, name="rec", tag="rec")
+        sgv = keep.tile([P, 1], F32, name="sgv", tag="sgv")
+        sgs = keep.tile([P, 1], F32, name="sgs", tag="sgs")
+
+        def load_w(c):
+            t = raw.tile([P, PACK, HL], BF16, name="w_raw", tag="raw")
+            nc.sync.dma_start(out=t[:], in_=W_down[:, c * HL:(c + 1) * HL].rearrange("(p j) h -> p j h", j=PACK))
+            return t
+
+        def load_rows(src, g):
+            t = raw.tile([P, PACK * D], BF16, name="rows_raw", tag="raw")
+            nc.sync.dma_start(out=t[:], in_=src[g * K_PASS:(g + 1) * K_PASS, :].rearrange("(p j) d -> p (j d)", j=PACK))
+            return t
+
+        def load_act(dst, src, c):
+            for g in range(G):
+                nc.sync.dma_start(
+                    out=dst[c][:, g * PACK:(g + 1) * PACK, :],
+                    in_=src[g * K_PASS:(g + 1) * K_PASS, c * HL:(c + 1) * HL].rearrange("(p t) h -> p t h", t=PACK),
+                )
+
+        w_raw = {}
+        e_raw = {}
+        x_raw = {}
+        w_raw[0] = load_w(0)
+        load_act(gate_sb, gate_pre, 0)
+        w_raw[1] = load_w(1)
+        e_raw[0] = load_rows(err, 0)
+        e_raw[1] = load_rows(err, 1)
+
+        nc.gpsimd.memset(warm_in[:], 0.0)
+        nc.scalar.activation(out=warm_out[:], in_=warm_in[:], func=ACT.Silu)
+        make_identity(nc, ident[:])
+        nc.gpsimd.memset(ones[:], 1.0)
+        nc.gpsimd.memset(ssq[:], 0.0)
+
+        def interleave(engine, src3):
+            t = grp.tile([P, HL * PACK], BF16, name="grouped", tag="grouped", align_bytes=64)
+            dst = t[:].rearrange("p (w j) -> p w j", j=PACK)
+            if engine == "v":
+                nc.vector.tensor_copy(out=dst, in_=src3.rearrange("p j w -> p w j"))
+            else:
+                nc.scalar.copy(out=dst, in_=src3.rearrange("p j w -> p w j"))
+            return t
+
+        def quantize(t, codes, scales, lo):
+            nc.vector.quantize_mx(
+                out=codes[:, lo:lo + HL].bitcast(FP8X4),
+                scales=scales[:, lo:lo + HL],
+                in_=t[:],
+            )
+
+        tanh_t, silu_m, silu_l, x_t, b_t = {}, {}, {}, {}, {}
+
+        def acts(b):
+            c, off = divmod(b * HB, HL)
+            src = gate_sb[c][:, :, off:off + HB]
+            silu_m[b] = elem.tile([P, G * PACK, HB], F32, name="silu_m", tag="silu_m")
+            nc.scalar.activation(out=silu_m[b][:], in_=src, func=ACT.Silu, scale=-1.0)
+            tanh_t[b] = elem.tile([P, G * PACK, HB], F32, name="tanh_t", tag="tanh_t")
+            nc.scalar.activation(out=tanh_t[b][:], in_=src, func=ACT.Tanh, scale=0.5)
+            silu_l[b] = elem.tile([P, G * PACK, HB], F32, name="silu_l", tag="silu_l")
+            nc.scalar.activation(out=silu_l[b][:], in_=src, func=ACT.Silu)
+
+        def xmul(b):
+            c, off = divmod(b * HB, HL)
+            x_t[b] = elem.tile([P, G * PACK, HB], F32, name="x_t", tag="x_t")
+            nc.vector.scalar_tensor_tensor(
+                out=x_t[b][:], in0=tanh_t[b][:], scalar=1.0, in1=up_sb[c][:, :, off:off + HB],
+                op0=ALU.add, op1=ALU.mult,
+            )
+
+        def bmul(b):
+            b_t[b] = elem.tile([P, G * PACK, HB], F32, name="b_t", tag="b_t")
+            nc.vector.scalar_tensor_tensor(
+                out=b_t[b][:], in0=silu_m[b][:], scalar=1.0, in1=x_t[b][:],
+                op0=ALU.subtract, op1=ALU.mult,
+            )
+
+        dh = {}
+
+        def stage1(u):
+            ht, g = divmod(u, G)
+            dh[u] = psum.tile([P, PACK, HT], BANK_DT, name="dh", tag="dh")
+            for t in range(PACK):
+                lo = g * K_PASS + t * P
+                nc.tensor.matmul_mx(
+                    out=dh[u][:, t, :],
+                    lhsT=e_codes[:, lo:lo + P].bitcast(FP8X4),
+                    lhsT_scale=e_scales[:, lo:lo + P],
+                    rhs=w_codes[:, ht * HT:(ht + 1) * HT].bitcast(FP8X4),
+                    rhs_scale=w_scales[:, ht * HT:(ht + 1) * HT],
+                    start=True, stop=True,
+                )
+
+        pq = {}
+
+        def pmul(u):
+            ht, g = divmod(u, G)
+            b, hl = divmod(ht, HB // HT)
+            if g == 0:
+                pq[ht] = prod.tile([P, 2, G, HT * PACK], BF16, name="pq", tag="pq", align_bytes=64)
+            bank = dh[u][:].rearrange("p t h -> p h t")
+            cols = slice(hl * HT, (hl + 1) * HT)
+            rows = slice(g * PACK, (g + 1) * PACK)
+            nc.vector.tensor_tensor(
+                out=pq[ht][:, 0, g, :].rearrange("p (h t) -> p h t", t=PACK),
+                in0=bank, in1=silu_l[b][:, rows, cols].rearrange("p t h -> p h t"), op=ALU.mult,
+            )
+            nc.vector.scalar_tensor_tensor(
+                out=pq[ht][:, 1, g, :].rearrange("p (h t) -> p h t", t=PACK),
+                in0=bank, scalar=-0.5, in1=b_t[b][:, rows, cols].rearrange("p t h -> p h t"),
+                op0=ALU.mult, op1=ALU.mult,
+            )
+
+        pc, ps = {}, {}
+
+        def pquant(ht):
+            pc[ht] = prod.tile([P, 2 * G * HT], U32, name="pc", tag="pc", align_bytes=64)
+            ps[ht] = prod.tile([P, 2 * G * HT], U8, name="ps", tag="ps", align_bytes=64)
+            nc.vector.quantize_mx(
+                out=pc[ht][:].bitcast(FP8X4), scales=ps[ht][:],
+                in_=pq[ht][:].rearrange("p a g c -> p (a g c)"),
+            )
+
+        def stage2(ht):
+            for a in range(2):
+                acc = psum.tile([P, D], F32, name="acc", tag="acc")
+                for g in range(G):
+                    lo = (a * G + g) * HT
+                    nc.tensor.matmul_mx(
+                        out=acc[:],
+                        lhsT=pc[ht][:, lo:lo + HT].bitcast(FP8X4),
+                        lhsT_scale=ps[ht][:, lo:lo + HT],
+                        rhs=x_codes[:, g * D:(g + 1) * D].bitcast(FP8X4),
+                        rhs_scale=x_scales[:, g * D:(g + 1) * D],
+                        start=(g == 0), stop=(g == G - 1),
+                    )
+                res = stage.tile([P, D], F32, name="res", tag="res")
+                if ht == N_HT - 1 and a == 1:
+                    nc.vector.tensor_scalar(out=res[:], in0=acc[:], scalar1=sgs[:, 0:1], scalar2=None, op0=ALU.mult)
+                else:
+                    nc.scalar.activation(out=res[:], in_=acc[:], func=ACT.Copy, scale=sgs[:, 0:1])
+                nc.sync.dma_start(out=outs[a][ht * HT:(ht + 1) * HT, :], in_=res[:])
+
+        gw0 = interleave("v", w_raw[0][:])
+        gw1 = interleave("v", w_raw[1][:])
+        quantize(gw0, w_codes, w_scales, 0)
+        quantize(gw1, w_codes, w_scales, HL)
+        acts(0)
+
+        w_raw[2] = load_w(2)
+        load_act(up_sb, up_pre, 0)
+        w_raw[3] = load_w(3)
+
+        e_grp = {}
+        for g in range(G):
+            words = e_raw[g][:].bitcast(F32)
+            e_grp[g] = grp.tile([P, HL * PACK], BF16, name="e_grouped", tag="grouped", align_bytes=64)
+            egw = e_grp[g][:].bitcast(F32).rearrange("p (t m u) -> p t m u", t=PACK, u=2)
+            for half in range(2):
+                xt = psum.tile([P, PACK, P], F32, name="xt", tag="dh")
+                for tt in range(2):
+                    t = 2 * half + tt
+                    for u in range(2):
+                        nc.tensor.transpose(
+                            out=xt[:, 2 * tt + u, :],
+                            in_=words[:, t * 256 + u:(t + 1) * 256:2],
+                            identity=ident[:],
+                        )
+                nc.scalar.copy(
+                    out=egw[:, 2 * half:2 * half + 2, :, :],
+                    in_=xt[:].rearrange("p (tt u) m -> p tt m u", u=2),
+                )
+        gram = psum.tile([P, P], F32, name="gram", tag="acc")
+        n_mm = G * PACK * (D // P)
+        i_mm = 0
+        for g in range(G):
+            for t in range(PACK):
+                for fb in range(D // P):
+                    blk = e_raw[g][:, t * D + fb * P:t * D + (fb + 1) * P]
+                    nc.tensor.matmul(out=gram[:], lhsT=blk, rhs=blk, start=(i_mm == 0), stop=(i_mm == n_mm - 1))
+                    i_mm += 1
+        for g in range(G):
+            quantize(e_grp[g], e_codes, e_scales, g * K_PASS)
+        nc.vector.scalar_tensor_tensor(
+            out=diag[:], in0=gram[:], scalar=1.0, in1=ident[:], op0=ALU.mult, op1=ALU.mult,
+            accum_out=ssq[:, 0:1],
+        )
+        tot = psum.tile([P, 2], F32, name="tot", tag="acc")
+        nc.tensor.matmul(out=tot[:], lhsT=ones[:], rhs=ssq[:], start=True, stop=True)
+
+        x_raw[0] = load_rows(x_pred, 0)
+        x_raw[1] = load_rows(x_pred, 1)
+        for c in range(1, N_HL):
+            load_act(gate_sb, gate_pre, c)
+            load_act(up_sb, up_pre, c)
+
+        acts(1)
+        nc.scalar.activation(out=em[:], in_=tot[:, 0:1], func=ACT.Sqrt, scale=1.0 / (N_TOK * N_TOK))
+        nc.gpsimd.tensor_scalar(out=ema[:], in0=em[:], scalar1=0.05, scalar2=0.95, op0=ALU.mult, op1=ALU.add)
+        nc.gpsimd.tensor_scalar(out=emc[:], in0=ema[:], scalar1=1e-8, scalar2=None, op0=ALU.max)
+        nc.vector.reciprocal(out=rec[:], in_=emc[:])
+        nc.gpsimd.tensor_scalar(out=sgv[:], in0=rec[:], scalar1=em[:, 0:1], scalar2=3.0, op0=ALU.mult, op1=ALU.min)
+        nc.gpsimd.tensor_scalar(out=sgs[:], in0=sgv[:], scalar1=1.0 / N_TOK, scalar2=None, op0=ALU.mult)
+
+        gx0 = interleave("s", x_raw[0][:].rearrange("p (j d) -> p j d", j=PACK))
+        gx1 = interleave("s", x_raw[1][:].rearrange("p (j d) -> p j d", j=PACK))
+        xmul(0)
+        quantize(gx0, x_codes, x_scales, 0)
+        bmul(0)
+        quantize(gx1, x_codes, x_scales, D)
+
+        N_U = N_HT * G
+        AHEAD = 4
+        for u in range(AHEAD):
+            stage1(u)
+        gw_late = {}
+        for b in range(N_HB):
+            for hl in range(HB // HT):
+                ht = b * (HB // HT) + hl
+                for g in range(G):
+                    u = ht * G + g
+                    pmul(u)
+                    if u + AHEAD < N_U:
+                        stage1(u + AHEAD)
+                if b + 1 < N_HB:
+                    if hl == 0:
+                        xmul(b + 1)
+                    else:
+                        bmul(b + 1)
+                pquant(ht)
+                if hl == 0 and b in (1, 2):
+                    quantize(gw_late[b + 1], w_codes, w_scales, (b + 1) * HL)
+                stage2(ht)
+            if b + 2 < N_HB:
+                acts(b + 2)
+            if b in (0, 1):
+                gw_late[b + 2] = interleave("s", w_raw[b + 2][:])

@@ -10,6 +10,7 @@ U8 = mybir.dt.uint8
 FP8X4 = mybir.dt.float8_e4m3fn_x4
 ACT = mybir.ActivationFunctionType
 ALU = mybir.AluOpType
+ENG = mybir.EngineType
 
 N_TOK, D, H = 1024, 512, 2048
 FLOPS = 3 * 2 * N_TOK * D * H
@@ -24,6 +25,7 @@ HB = 256
 N_HB = H // HB
 HL = 512
 N_HL = H // HL
+NQ = G * PACK // 2
 BANK_DT = F32
 
 
@@ -35,7 +37,7 @@ def tile_continuummemorysystem_pa_kernel(tc, err, W_down, gate_pre, up_pre, x_pr
         keep = ctx.enter_context(tc.tile_pool(name="keep", bufs=1))
         raw = ctx.enter_context(tc.tile_pool(name="raw", bufs=4))
         grp = ctx.enter_context(tc.tile_pool(name="grp", bufs=3))
-        elem = ctx.enter_context(tc.tile_pool(name="elem", bufs=2))
+        elem = ctx.enter_context(tc.tile_pool(name="elem", bufs=3))
         prod = ctx.enter_context(tc.tile_pool(name="prod", bufs=3))
         stage = ctx.enter_context(tc.tile_pool(name="stage", bufs=4))
         psum = ctx.enter_context(tc.psum_pool(name="psum", bufs=4))
@@ -78,28 +80,29 @@ def tile_continuummemorysystem_pa_kernel(tc, err, W_down, gate_pre, up_pre, x_pr
                     in_=src[g * K_PASS:(g + 1) * K_PASS, c * HL:(c + 1) * HL].rearrange("(p t) h -> p t h", t=PACK),
                 )
 
-        w_raw = {}
-        e_raw = {}
-        x_raw = {}
-        w_raw[0] = load_w(0)
+        w_raw, e_raw, x_raw = {}, {}, {}
         load_act(gate_sb, gate_pre, 0)
-        w_raw[1] = load_w(1)
+        w_raw[0] = load_w(0)
         e_raw[0] = load_rows(err, 0)
         e_raw[1] = load_rows(err, 1)
+        load_act(gate_sb, gate_pre, 1)
+        load_act(up_sb, up_pre, 0)
+        w_raw[1] = load_w(1)
 
         nc.gpsimd.memset(warm_in[:], 0.0)
-        nc.scalar.activation(out=warm_out[:], in_=warm_in[:], func=ACT.Silu)
+        nc.scalar.activation(out=warm_out[:], in_=warm_in[:], func=ACT.Sigmoid)
         make_identity(nc, ident[:])
         nc.gpsimd.memset(ones[:], 1.0)
         nc.gpsimd.memset(ssq[:], 0.0)
 
         def interleave(engine, src3):
             t = grp.tile([P, HL * PACK], BF16, name="grouped", tag="grouped", align_bytes=64)
-            dst = t[:].rearrange("p (w j) -> p w j", j=PACK)
+            dst = t[:].rearrange("p (c i j) -> p c j i", i=4, j=PACK)
+            src = src3.rearrange("p j (c i) -> p c j i", i=4)
             if engine == "v":
-                nc.vector.tensor_copy(out=dst, in_=src3.rearrange("p j w -> p w j"))
+                nc.vector.tensor_copy(out=dst, in_=src)
             else:
-                nc.scalar.copy(out=dst, in_=src3.rearrange("p j w -> p w j"))
+                nc.scalar.copy(out=dst, in_=src)
             return t
 
         def quantize(t, codes, scales, lo):
@@ -109,30 +112,37 @@ def tile_continuummemorysystem_pa_kernel(tc, err, W_down, gate_pre, up_pre, x_pr
                 in_=t[:],
             )
 
-        tanh_t, silu_m, silu_l, x_t, b_t = {}, {}, {}, {}, {}
-
-        def acts(b):
+        def gate_pairs(b):
             c, off = divmod(b * HB, HL)
-            src = gate_sb[c][:, :, off:off + HB]
-            silu_m[b] = elem.tile([P, G * PACK, HB], F32, name="silu_m", tag="silu_m")
-            nc.scalar.activation(out=silu_m[b][:], in_=src, func=ACT.Silu, scale=-1.0)
-            tanh_t[b] = elem.tile([P, G * PACK, HB], F32, name="tanh_t", tag="tanh_t")
-            nc.scalar.activation(out=tanh_t[b][:], in_=src, func=ACT.Tanh, scale=0.5)
-            silu_l[b] = elem.tile([P, G * PACK, HB], F32, name="silu_l", tag="silu_l")
-            nc.scalar.activation(out=silu_l[b][:], in_=src, func=ACT.Silu)
+            return gate_sb[c][:, :, off:off + HB].rearrange("p (q e) h -> p q h e", e=2)
+
+        sx, mb, lt = {}, {}, {}
+
+        def act_sig(b):
+            sx[b] = elem.tile([P, NQ, HB, 2], F32, name="sx", tag="sx", bufs=5)
+            nc.scalar.activation(out=sx[b][:], in_=gate_pairs(b), func=ACT.Sigmoid)
+
+        def act_m(b):
+            mb[b] = elem.tile([P, NQ, HB, 2], F32, name="mb", tag="mb")
+            nc.scalar.activation(out=mb[b][:], in_=gate_pairs(b), func=ACT.Silu, scale=-1.0)
+
+        def act_l(b):
+            lt[b] = elem.tile([P, NQ, HB, 2], F32, name="lt", tag="lt")
+            nc.scalar.activation(out=lt[b][:], in_=gate_pairs(b), func=ACT.Silu)
 
         def xmul(b):
             c, off = divmod(b * HB, HL)
-            x_t[b] = elem.tile([P, G * PACK, HB], F32, name="x_t", tag="x_t")
-            nc.vector.scalar_tensor_tensor(
-                out=x_t[b][:], in0=tanh_t[b][:], scalar=1.0, in1=up_sb[c][:, :, off:off + HB],
-                op0=ALU.add, op1=ALU.mult,
-            )
+            for q in range(NQ):
+                nc.vector.scalar_tensor_tensor(
+                    out=sx[b][:, q, :, :], in0=sx[b][:, q, :, :], scalar=-1.0,
+                    in1=up_sb[c][:, 2 * q:2 * q + 2, off:off + HB].rearrange("p e h -> p h e"),
+                    op0=ALU.mult, op1=ALU.mult,
+                )
 
         def bmul(b):
-            b_t[b] = elem.tile([P, G * PACK, HB], F32, name="b_t", tag="b_t")
+            flat = mb[b][:].rearrange("p q h e -> p (q h e)")
             nc.vector.scalar_tensor_tensor(
-                out=b_t[b][:], in0=silu_m[b][:], scalar=1.0, in1=x_t[b][:],
+                out=flat, in0=flat, scalar=1.0, in1=sx[b][:].rearrange("p q h e -> p (q h e)"),
                 op0=ALU.subtract, op1=ALU.mult,
             )
 
@@ -159,18 +169,14 @@ def tile_continuummemorysystem_pa_kernel(tc, err, W_down, gate_pre, up_pre, x_pr
             b, hl = divmod(ht, HB // HT)
             if g == 0:
                 pq[ht] = prod.tile([P, 2, G, HT * PACK], BF16, name="pq", tag="pq", align_bytes=64)
-            bank = dh[u][:].rearrange("p t h -> p h t")
+            bank = dh[u][:].rearrange("p (s e) h -> p h s e", e=2)
             cols = slice(hl * HT, (hl + 1) * HT)
-            rows = slice(g * PACK, (g + 1) * PACK)
-            nc.vector.tensor_tensor(
-                out=pq[ht][:, 0, g, :].rearrange("p (h t) -> p h t", t=PACK),
-                in0=bank, in1=silu_l[b][:, rows, cols].rearrange("p t h -> p h t"), op=ALU.mult,
-            )
-            nc.vector.scalar_tensor_tensor(
-                out=pq[ht][:, 1, g, :].rearrange("p (h t) -> p h t", t=PACK),
-                in0=bank, scalar=-0.5, in1=b_t[b][:, rows, cols].rearrange("p t h -> p h t"),
-                op0=ALU.mult, op1=ALU.mult,
-            )
+            prs = slice(2 * g, 2 * g + 2)
+            for a, factor in ((0, lt[b]), (1, mb[b])):
+                nc.vector.tensor_tensor(
+                    out=pq[ht][:, a, g, :].rearrange("p (h s e) -> p h s e", s=2, e=2),
+                    in0=bank, in1=factor[:, prs, cols, :].rearrange("p s h e -> p h s e"), op=ALU.mult,
+                )
 
         pc, ps = {}, {}
 
@@ -182,35 +188,36 @@ def tile_continuummemorysystem_pa_kernel(tc, err, W_down, gate_pre, up_pre, x_pr
                 in_=pq[ht][:].rearrange("p a g c -> p (a g c)"),
             )
 
+        acc = {}
+
         def stage2(ht):
             for a in range(2):
-                acc = psum.tile([P, D], F32, name="acc", tag="acc")
+                acc[ht, a] = psum.tile([P, D], F32, name="acc", tag="acc")
                 for g in range(G):
                     lo = (a * G + g) * HT
                     nc.tensor.matmul_mx(
-                        out=acc[:],
+                        out=acc[ht, a][:],
                         lhsT=pc[ht][:, lo:lo + HT].bitcast(FP8X4),
                         lhsT_scale=ps[ht][:, lo:lo + HT],
                         rhs=x_codes[:, g * D:(g + 1) * D].bitcast(FP8X4),
                         rhs_scale=x_scales[:, g * D:(g + 1) * D],
                         start=(g == 0), stop=(g == G - 1),
                     )
+
+        def evac(ht):
+            for a in range(2):
                 res = stage.tile([P, D], F32, name="res", tag="res")
                 if ht == N_HT - 1 and a == 1:
-                    nc.vector.tensor_scalar(out=res[:], in0=acc[:], scalar1=sgs[:, 0:1], scalar2=None, op0=ALU.mult)
+                    nc.vector.tensor_scalar(out=res[:], in0=acc[ht, a][:], scalar1=sgs[:, 0:1], scalar2=None, op0=ALU.mult)
                 else:
-                    nc.scalar.activation(out=res[:], in_=acc[:], func=ACT.Copy, scale=sgs[:, 0:1])
+                    nc.scalar.activation(out=res[:], in_=acc[ht, a][:], func=ACT.Copy, scale=sgs[:, 0:1])
                 nc.sync.dma_start(out=outs[a][ht * HT:(ht + 1) * HT, :], in_=res[:])
 
-        gw0 = interleave("v", w_raw[0][:])
-        gw1 = interleave("v", w_raw[1][:])
-        quantize(gw0, w_codes, w_scales, 0)
-        quantize(gw1, w_codes, w_scales, HL)
-        acts(0)
+        ctx.enter_context(tc.manual_schedule(engines={ENG.Activation, ENG.DVE}))
 
-        w_raw[2] = load_w(2)
-        load_act(up_sb, up_pre, 0)
-        w_raw[3] = load_w(3)
+        act_sig(0)
+        act_sig(1)
+        gw0 = interleave("v", w_raw[0][:])
 
         e_grp = {}
         for g in range(G):
@@ -231,6 +238,7 @@ def tile_continuummemorysystem_pa_kernel(tc, err, W_down, gate_pre, up_pre, x_pr
                     out=egw[:, 2 * half:2 * half + 2, :, :],
                     in_=xt[:].rearrange("p (tt u) m -> p tt m u", u=2),
                 )
+        quantize(gw0, w_codes, w_scales, 0)
         gram = psum.tile([P, P], F32, name="gram", tag="acc")
         n_mm = G * PACK * (D // P)
         i_mm = 0
@@ -240,6 +248,8 @@ def tile_continuummemorysystem_pa_kernel(tc, err, W_down, gate_pre, up_pre, x_pr
                     blk = e_raw[g][:, t * D + fb * P:t * D + (fb + 1) * P]
                     nc.tensor.matmul(out=gram[:], lhsT=blk, rhs=blk, start=(i_mm == 0), stop=(i_mm == n_mm - 1))
                     i_mm += 1
+        act_sig(2)
+        act_sig(3)
         for g in range(G):
             quantize(e_grp[g], e_codes, e_scales, g * K_PASS)
         nc.vector.scalar_tensor_tensor(
@@ -251,48 +261,78 @@ def tile_continuummemorysystem_pa_kernel(tc, err, W_down, gate_pre, up_pre, x_pr
 
         x_raw[0] = load_rows(x_pred, 0)
         x_raw[1] = load_rows(x_pred, 1)
-        for c in range(1, N_HL):
-            load_act(gate_sb, gate_pre, c)
-            load_act(up_sb, up_pre, c)
+        load_act(up_sb, up_pre, 1)
+        load_act(gate_sb, gate_pre, 2)
+        load_act(up_sb, up_pre, 2)
+        w_raw[2] = load_w(2)
+        load_act(gate_sb, gate_pre, 3)
+        load_act(up_sb, up_pre, 3)
+        w_raw[3] = load_w(3)
 
-        acts(1)
+        xmul(0)
+        xmul(1)
         nc.scalar.activation(out=em[:], in_=tot[:, 0:1], func=ACT.Sqrt, scale=1.0 / (N_TOK * N_TOK))
         nc.gpsimd.tensor_scalar(out=ema[:], in0=em[:], scalar1=0.05, scalar2=0.95, op0=ALU.mult, op1=ALU.add)
         nc.gpsimd.tensor_scalar(out=emc[:], in0=ema[:], scalar1=1e-8, scalar2=None, op0=ALU.max)
+        act_m(0)
+        act_l(0)
+        gw1 = interleave("v", w_raw[1][:])
         nc.vector.reciprocal(out=rec[:], in_=emc[:])
+        quantize(gw1, w_codes, w_scales, HL)
         nc.gpsimd.tensor_scalar(out=sgv[:], in0=rec[:], scalar1=em[:, 0:1], scalar2=3.0, op0=ALU.mult, op1=ALU.min)
         nc.gpsimd.tensor_scalar(out=sgs[:], in0=sgv[:], scalar1=1.0 / N_TOK, scalar2=None, op0=ALU.mult)
-
         gx0 = interleave("s", x_raw[0][:].rearrange("p (j d) -> p j d", j=PACK))
         gx1 = interleave("s", x_raw[1][:].rearrange("p (j d) -> p j d", j=PACK))
-        xmul(0)
-        quantize(gx0, x_codes, x_scales, 0)
+        act_m(1)
+        act_l(1)
+        xmul(2)
+        xmul(3)
         bmul(0)
-        quantize(gx1, x_codes, x_scales, D)
 
         N_U = N_HT * G
         AHEAD = 4
+        gw_late = {}
         for u in range(AHEAD):
             stage1(u)
-        gw_late = {}
-        for b in range(N_HB):
-            for hl in range(HB // HT):
-                ht = b * (HB // HT) + hl
-                for g in range(G):
-                    u = ht * G + g
-                    pmul(u)
-                    if u + AHEAD < N_U:
-                        stage1(u + AHEAD)
-                if b + 1 < N_HB:
-                    if hl == 0:
-                        xmul(b + 1)
-                    else:
-                        bmul(b + 1)
-                pquant(ht)
-                if hl == 0 and b in (1, 2):
+        for u in range(N_U):
+            b, r = divmod(u, 4)
+            ht = u // G
+            pmul(u)
+            if u + AHEAD < N_U:
+                stage1(u + AHEAD)
+            if u == 0:
+                quantize(gx0, x_codes, x_scales, 0)
+            if u == 1:
+                quantize(gx1, x_codes, x_scales, D)
+            if r % 2 == 0 and ht >= 1:
+                pquant(ht - 1)
+                stage2(ht - 1)
+            if r == 0:
+                if u == 12:
+                    act_sig(7)
+                if b + 2 < N_HB:
+                    act_m(b + 2)
+            if r == 1:
+                if b >= 1:
+                    evac(2 * b - 1)
+                if 4 <= b + 1 < N_HB:
+                    xmul(b + 1)
+            if r == 2:
+                if b + 2 < N_HB:
+                    act_l(b + 2)
+                if u == 10:
+                    act_sig(4)
+                if b in (1, 2):
                     quantize(gw_late[b + 1], w_codes, w_scales, (b + 1) * HL)
-                stage2(ht)
-            if b + 2 < N_HB:
-                acts(b + 2)
-            if b in (0, 1):
-                gw_late[b + 2] = interleave("s", w_raw[b + 2][:])
+                if b + 1 < N_HB:
+                    bmul(b + 1)
+            if r == 3:
+                evac(2 * b)
+                if b in (0, 1):
+                    gw_late[b + 2] = interleave("s", w_raw[b + 2][:])
+                if u == 11:
+                    act_sig(5)
+                    act_sig(6)
+        pquant(N_HT - 1)
+        stage2(N_HT - 1)
+        evac(N_HT - 1)

@@ -73,16 +73,17 @@ def tile_continuummemorysystem_pa_kernel(tc, err, W_down, gate_pre, up_pre, x_pr
             nc.sync.dma_start(out=t[:], in_=src[g * K_PASS:(g + 1) * K_PASS, :].rearrange("(p j) d -> p (j d)", j=PACK))
             return t
 
-        def load_act(dst, src, c):
+        def load_act(dst, src, c, lo=0, hi=HL):
             for g in range(G):
                 nc.sync.dma_start(
-                    out=dst[c][:, g * PACK:(g + 1) * PACK, :],
-                    in_=src[g * K_PASS:(g + 1) * K_PASS, c * HL:(c + 1) * HL].rearrange("(p t) h -> p t h", t=PACK),
+                    out=dst[c][:, g * PACK:(g + 1) * PACK, lo:hi],
+                    in_=src[g * K_PASS:(g + 1) * K_PASS, c * HL + lo:c * HL + hi].rearrange("(p t) h -> p t h", t=PACK),
                 )
 
         w_raw, e_raw, x_raw = {}, {}, {}
-        load_act(gate_sb, gate_pre, 0)
+        load_act(gate_sb, gate_pre, 0, 0, HB)
         w_raw[0] = load_w(0)
+        load_act(gate_sb, gate_pre, 0, HB, HL)
         e_raw[0] = load_rows(err, 0)
         e_raw[1] = load_rows(err, 1)
         load_act(gate_sb, gate_pre, 1)
@@ -104,6 +105,14 @@ def tile_continuummemorysystem_pa_kernel(tc, err, W_down, gate_pre, up_pre, x_pr
             else:
                 nc.scalar.copy(out=dst, in_=src)
             return t
+
+        def interleave_half(t, src3, half):
+            for lo in (half * 256, half * 256 + 128):
+                nc.gpsimd.tensor_scalar(
+                    out=t[:, lo * PACK:(lo + 128) * PACK].rearrange("p (w j) -> p w j", j=PACK),
+                    in0=src3[:, :, lo:lo + 128].rearrange("p j w -> p w j"),
+                    scalar1=1.0, scalar2=0.0, op0=ALU.mult, op1=ALU.add,
+                )
 
         def quantize(t, codes, scales, lo):
             nc.vector.quantize_mx(
@@ -162,18 +171,38 @@ def tile_continuummemorysystem_pa_kernel(tc, err, W_down, gate_pre, up_pre, x_pr
                     start=True, stop=True,
                 )
 
-        pq = {}
+        pq, dhs = {}, {}
+
+        def new_pq(ht):
+            pq[ht] = prod.tile([P, 2, G, HT * PACK], BF16, name="pq", tag="pq", align_bytes=64)
 
         def pmul(u):
             ht, g = divmod(u, G)
             b, hl = divmod(ht, HB // HT)
-            if g == 0:
-                pq[ht] = prod.tile([P, 2, G, HT * PACK], BF16, name="pq", tag="pq", align_bytes=64)
             bank = dh[u][:].rearrange("p (s e) h -> p h s e", e=2)
             cols = slice(hl * HT, (hl + 1) * HT)
             prs = slice(2 * g, 2 * g + 2)
             for a, factor in ((0, lt[b]), (1, mb[b])):
                 nc.vector.tensor_tensor(
+                    out=pq[ht][:, a, g, :].rearrange("p (h s e) -> p h s e", s=2, e=2),
+                    in0=bank, in1=factor[:, prs, cols, :].rearrange("p s h e -> p h s e"), op=ALU.mult,
+                )
+
+        def dhcopy(u):
+            dhs[u] = prod.tile([P, HT * PACK], BANK_DT, name="dhs", tag="dhs", bufs=2)
+            nc.scalar.copy(
+                out=dhs[u][:].rearrange("p (h t) -> p h t", t=PACK),
+                in_=dh[u][:].rearrange("p t h -> p h t"),
+            )
+
+        def gp_pmul(u):
+            ht, g = divmod(u, G)
+            b, hl = divmod(ht, HB // HT)
+            bank = dhs[u][:].rearrange("p (h s e) -> p h s e", s=2, e=2)
+            cols = slice(hl * HT, (hl + 1) * HT)
+            prs = slice(2 * g, 2 * g + 2)
+            for a, factor in ((1, mb[b]), (0, lt[b])):
+                nc.gpsimd.tensor_tensor(
                     out=pq[ht][:, a, g, :].rearrange("p (h s e) -> p h s e", s=2, e=2),
                     in0=bank, in1=factor[:, prs, cols, :].rearrange("p s h e -> p h s e"), op=ALU.mult,
                 )
@@ -204,16 +233,15 @@ def tile_continuummemorysystem_pa_kernel(tc, err, W_down, gate_pre, up_pre, x_pr
                         start=(g == 0), stop=(g == G - 1),
                     )
 
-        def evac(ht):
-            for a in range(2):
-                res = stage.tile([P, D], F32, name="res", tag="res")
-                if ht == N_HT - 1 and a == 1:
-                    nc.vector.tensor_scalar(out=res[:], in0=acc[ht, a][:], scalar1=sgs[:, 0:1], scalar2=None, op0=ALU.mult)
-                else:
-                    nc.scalar.activation(out=res[:], in_=acc[ht, a][:], func=ACT.Copy, scale=sgs[:, 0:1])
-                nc.sync.dma_start(out=outs[a][ht * HT:(ht + 1) * HT, :], in_=res[:])
+        def evac(engine, ht, a):
+            res = stage.tile([P, D], F32, name="res", tag="res")
+            if engine == "v":
+                nc.vector.tensor_scalar(out=res[:], in0=acc[ht, a][:], scalar1=sgs[:, 0:1], scalar2=None, op0=ALU.mult)
+            else:
+                nc.scalar.activation(out=res[:], in_=acc[ht, a][:], func=ACT.Copy, scale=sgs[:, 0:1])
+            nc.sync.dma_start(out=outs[a][ht * HT:(ht + 1) * HT, :], in_=res[:])
 
-        ctx.enter_context(tc.manual_schedule(engines={ENG.Activation, ENG.DVE}))
+        ctx.enter_context(tc.manual_schedule(engines={ENG.Activation, ENG.DVE, ENG.Pool}))
 
         act_sig(0)
         act_sig(1)
@@ -276,63 +304,69 @@ def tile_continuummemorysystem_pa_kernel(tc, err, W_down, gate_pre, up_pre, x_pr
         nc.gpsimd.tensor_scalar(out=emc[:], in0=ema[:], scalar1=1e-8, scalar2=None, op0=ALU.max)
         act_m(0)
         act_l(0)
+        stage1(3)
+        dhcopy(3)
         gw1 = interleave("v", w_raw[1][:])
         nc.vector.reciprocal(out=rec[:], in_=emc[:])
         quantize(gw1, w_codes, w_scales, HL)
         nc.gpsimd.tensor_scalar(out=sgv[:], in0=rec[:], scalar1=em[:, 0:1], scalar2=3.0, op0=ALU.mult, op1=ALU.min)
         nc.gpsimd.tensor_scalar(out=sgs[:], in0=sgv[:], scalar1=1.0 / N_TOK, scalar2=None, op0=ALU.mult)
-        gx0 = interleave("s", x_raw[0][:].rearrange("p (j d) -> p j d", j=PACK))
-        gx1 = interleave("s", x_raw[1][:].rearrange("p (j d) -> p j d", j=PACK))
+        gx0 = interleave("v", x_raw[0][:].rearrange("p (j d) -> p j d", j=PACK))
+        gx1 = interleave("v", x_raw[1][:].rearrange("p (j d) -> p j d", j=PACK))
+        quantize(gx0, x_codes, x_scales, 0)
+        quantize(gx1, x_codes, x_scales, D)
         act_m(1)
         act_l(1)
-        xmul(2)
-        xmul(3)
         bmul(0)
 
-        N_U = N_HT * G
-        AHEAD = 4
         gw_late = {}
-        for u in range(AHEAD):
+        for u in range(3):
             stage1(u)
-        for u in range(N_U):
-            b, r = divmod(u, 4)
-            ht = u // G
-            pmul(u)
-            if u + AHEAD < N_U:
-                stage1(u + AHEAD)
-            if u == 0:
-                quantize(gx0, x_codes, x_scales, 0)
-            if u == 1:
-                quantize(gx1, x_codes, x_scales, D)
-            if r % 2 == 0 and ht >= 1:
-                pquant(ht - 1)
-                stage2(ht - 1)
-            if r == 0:
-                if u == 12:
-                    act_sig(7)
-                if b + 2 < N_HB:
-                    act_m(b + 2)
-            if r == 1:
-                if b >= 1:
-                    evac(2 * b - 1)
-                if 4 <= b + 1 < N_HB:
-                    xmul(b + 1)
-            if r == 2:
-                if b + 2 < N_HB:
-                    act_l(b + 2)
-                if u == 10:
-                    act_sig(4)
-                if b in (1, 2):
-                    quantize(gw_late[b + 1], w_codes, w_scales, (b + 1) * HL)
-                if b + 1 < N_HB:
-                    bmul(b + 1)
-            if r == 3:
-                evac(2 * b)
-                if b in (0, 1):
-                    gw_late[b + 2] = interleave("s", w_raw[b + 2][:])
-                if u == 11:
-                    act_sig(5)
-                    act_sig(6)
-        pquant(N_HT - 1)
-        stage2(N_HT - 1)
-        evac(N_HT - 1)
+        for b in range(N_HB):
+            u0 = 4 * b
+            ht0, ht1 = 2 * b, 2 * b + 1
+            more = b + 1 < N_HB
+            new_pq(ht0)
+            new_pq(ht1)
+            gp_pmul(u0 + 3)
+            if b < 4:
+                c_late, half = 2 + b // 2, b % 2
+                if half == 0:
+                    gw_late[c_late] = grp.tile([P, HL * PACK], BF16, name="grouped", tag="grouped", align_bytes=64)
+                interleave_half(gw_late[c_late], w_raw[c_late], half)
+            if more:
+                stage1(u0 + 7)
+                dhcopy(u0 + 7)
+            if b >= 1:
+                evac("s", ht0 - 1, 0)
+                evac("s", ht0 - 1, 1)
+            if b == 3:
+                act_sig(7)
+            if b + 2 < N_HB:
+                act_m(b + 2)
+                act_l(b + 2)
+            if b == 2:
+                act_sig(4)
+            for i in range(3):
+                pmul(u0 + i)
+                if more:
+                    stage1(u0 + 4 + i)
+            pquant(ht0)
+            stage2(ht0)
+            if b < 2:
+                xmul(b + 2)
+            if 4 <= b + 1 < N_HB:
+                xmul(b + 1)
+            if b in (2, 4):
+                quantize(gw_late[1 + b // 2], w_codes, w_scales, (1 + b // 2) * HL)
+            pquant(ht1)
+            stage2(ht1)
+            if more:
+                bmul(b + 1)
+            evac("s", ht0, 0)
+            evac("s", ht0, 1)
+            if b == 2:
+                act_sig(5)
+                act_sig(6)
+        evac("s", N_HT - 1, 0)
+        evac("v", N_HT - 1, 1)

from contextlib import ExitStack

import concourse.mybir as mybir
from concourse.masks import make_identity

F32 = mybir.dt.float32
BF16 = mybir.dt.bfloat16
U32 = mybir.dt.uint32
U8 = mybir.dt.uint8
FP8X4 = mybir.dt.float8_e4m3fn_x4
ACT = mybir.ActivationFunctionType
ALU = mybir.AluOpType
ENG = mybir.EngineType

N_TOK, D, H = 1024, 512, 2048
FLOPS = 3 * 2 * N_TOK * D * H

P = 128
PACK = 4
K_PASS = P * PACK
G = N_TOK // K_PASS
HT = 128
N_HT = H // HT
HB = 256
N_HB = H // HB
HL = 512
N_HL = H // HL
NQ = G * PACK // 2
BANK_DT = F32


def tile_continuummemorysystem_pa_kernel(tc, err, W_down, gate_pre, up_pre, x_pred, out_0, out_1):
    nc = tc.nc
    outs = (out_0, out_1)

    with ExitStack() as ctx:
        keep = ctx.enter_context(tc.tile_pool(name="keep", bufs=1))
        raw = ctx.enter_context(tc.tile_pool(name="raw", bufs=4))
        grp = ctx.enter_context(tc.tile_pool(name="grp", bufs=3))
        elem = ctx.enter_context(tc.tile_pool(name="elem", bufs=3))
        prod = ctx.enter_context(tc.tile_pool(name="prod", bufs=3))
        stage = ctx.enter_context(tc.tile_pool(name="stage", bufs=4))
        psum = ctx.enter_context(tc.psum_pool(name="psum", bufs=4))

        gate_sb = [keep.tile([P, G * PACK, HL], BF16, name="gate%d" % c, tag="gate%d" % c) for c in range(N_HL)]
        up_sb = [keep.tile([P, G * PACK, HL], BF16, name="up%d" % c, tag="up%d" % c) for c in range(N_HL)]
        w_codes = keep.tile([P, H], U32, name="w_codes", tag="w_codes", align_bytes=64)
        w_scales = keep.tile([P, H], U8, name="w_scales", tag="w_scales", align_bytes=64)
        e_codes = keep.tile([P, N_TOK], U32, name="e_codes", tag="e_codes", align_bytes=64)
        e_scales = keep.tile([P, N_TOK], U8, name="e_scales", tag="e_scales", align_bytes=64)
        x_codes = keep.tile([P, G * D], U32, name="x_codes", tag="x_codes", align_bytes=64)
        x_scales = keep.tile([P, G * D], U8, name="x_scales", tag="x_scales", align_bytes=64)
        ident = keep.tile([P, P], F32, name="ident", tag="ident")
        ones = keep.tile([P, P], F32, name="ones", tag="ones")
        diag = keep.tile([P, P], F32, name="diag", tag="diag")
        ssq = keep.tile([P, 2], F32, name="ssq", tag="ssq")
        warm_in = keep.tile([P, 1], F32, name="warm_in", tag="warm_in")
        warm_out = keep.tile([P, 1], F32, name="warm_out", tag="warm_out")
        em = keep.tile([P, 1], F32, name="em", tag="em")
        ema = keep.tile([P, 1], F32, name="ema", tag="ema")
        emc = keep.tile([P, 1], F32, name="emc", tag="emc")
        rec = keep.tile([P, 1], F32, name="rec", tag="rec")
        sgv = keep.tile([P, 1], F32, name="sgv", tag="sgv")
        sgs = keep.tile([P, 1], F32, name="sgs", tag="sgs")

        def load_w(c):
            t = raw.tile([P, PACK, HL], BF16, name="w_raw", tag="raw")
            nc.sync.dma_start(out=t[:], in_=W_down[:, c * HL:(c + 1) * HL].rearrange("(p j) h -> p j h", j=PACK))
            return t

        def load_rows(src, g):
            t = raw.tile([P, PACK * D], BF16, name="rows_raw", tag="raw")
            nc.sync.dma_start(out=t[:], in_=src[g * K_PASS:(g + 1) * K_PASS, :].rearrange("(p j) d -> p (j d)", j=PACK))
            return t

        def load_act(dst, src, c, lo=0, hi=HL):
            for g in range(G):
                nc.sync.dma_start(
                    out=dst[c][:, g * PACK:(g + 1) * PACK, lo:hi],
                    in_=src[g * K_PASS:(g + 1) * K_PASS, c * HL + lo:c * HL + hi].rearrange("(p t) h -> p t h", t=PACK),
                )

        w_raw, e_raw, x_raw = {}, {}, {}
        load_act(gate_sb, gate_pre, 0, 0, HB)
        w_raw[0] = load_w(0)
        load_act(gate_sb, gate_pre, 0, HB, HL)
        e_raw[0] = load_rows(err, 0)
        e_raw[1] = load_rows(err, 1)
        load_act(gate_sb, gate_pre, 1)
        load_act(up_sb, up_pre, 0)
        w_raw[1] = load_w(1)

        nc.gpsimd.memset(warm_in[:], 0.0)
        nc.scalar.activation(out=warm_out[:], in_=warm_in[:], func=ACT.Sigmoid)
        make_identity(nc, ident[:])
        nc.gpsimd.memset(ones[:], 1.0)
        nc.gpsimd.memset(ssq[:], 0.0)

        def interleave(engine, src3):
            t = grp.tile([P, HL * PACK], BF16, name="grouped", tag="grouped", align_bytes=64)
            dst = t[:].rearrange("p (c i j) -> p c j i", i=4, j=PACK)
            src = src3.rearrange("p j (c i) -> p c j i", i=4)
            if engine == "v":
                nc.vector.tensor_copy(out=dst, in_=src)
            else:
                nc.scalar.copy(out=dst, in_=src)
            return t

        def interleave_half(t, src3, half):
            for lo in (half * 256, half * 256 + 128):
                nc.gpsimd.tensor_scalar(
                    out=t[:, lo * PACK:(lo + 128) * PACK].rearrange("p (w j) -> p w j", j=PACK),
                    in0=src3[:, :, lo:lo + 128].rearrange("p j w -> p w j"),
                    scalar1=1.0, scalar2=0.0, op0=ALU.mult, op1=ALU.add,
                )

        def quantize(t, codes, scales, lo):
            nc.vector.quantize_mx(
                out=codes[:, lo:lo + HL].bitcast(FP8X4),
                scales=scales[:, lo:lo + HL],
                in_=t[:],
            )

        def gate_pairs(b):
            c, off = divmod(b * HB, HL)
            return gate_sb[c][:, :, off:off + HB].rearrange("p (q e) h -> p q h e", e=2)

        sx, mb, lt = {}, {}, {}

        def act_sig(b):
            sx[b] = elem.tile([P, NQ, HB, 2], F32, name="sx", tag="sx", bufs=5)
            nc.scalar.activation(out=sx[b][:], in_=gate_pairs(b), func=ACT.Sigmoid)

        def act_m(b):
            mb[b] = elem.tile([P, NQ, HB, 2], F32, name="mb", tag="mb")
            nc.scalar.activation(out=mb[b][:], in_=gate_pairs(b), func=ACT.Silu, scale=-1.0)

        def act_l(b):
            lt[b] = elem.tile([P, NQ, HB, 2], F32, name="lt", tag="lt")
            nc.scalar.activation(out=lt[b][:], in_=gate_pairs(b), func=ACT.Silu)

        def xmul(b):
            c, off = divmod(b * HB, HL)
            for q in range(NQ):
                nc.vector.scalar_tensor_tensor(
                    out=sx[b][:, q, :, :], in0=sx[b][:, q, :, :], scalar=-1.0,
                    in1=up_sb[c][:, 2 * q:2 * q + 2, off:off + HB].rearrange("p e h -> p h e"),
                    op0=ALU.mult, op1=ALU.mult,
                )

        def bmul(b):
            flat = mb[b][:].rearrange("p q h e -> p (q h e)")
            nc.vector.scalar_tensor_tensor(
                out=flat, in0=flat, scalar=1.0, in1=sx[b][:].rearrange("p q h e -> p (q h e)"),
                op0=ALU.subtract, op1=ALU.mult,
            )

        dh = {}

        def stage1(u):
            ht, g = divmod(u, G)
            dh[u] = psum.tile([P, PACK, HT], BANK_DT, name="dh", tag="dh")
            for t in range(PACK):
                lo = g * K_PASS + t * P
                nc.tensor.matmul_mx(
                    out=dh[u][:, t, :],
                    lhsT=e_codes[:, lo:lo + P].bitcast(FP8X4),
                    lhsT_scale=e_scales[:, lo:lo + P],
                    rhs=w_codes[:, ht * HT:(ht + 1) * HT].bitcast(FP8X4),
                    rhs_scale=w_scales[:, ht * HT:(ht + 1) * HT],
                    start=True, stop=True,
                )

        pq, dhs = {}, {}

        def new_pq(ht):
            pq[ht] = prod.tile([P, 2, G, HT * PACK], BF16, name="pq", tag="pq", align_bytes=64)

        def pmul(u):
            ht, g = divmod(u, G)
            b, hl = divmod(ht, HB // HT)
            bank = dh[u][:].rearrange("p (s e) h -> p h s e", e=2)
            cols = slice(hl * HT, (hl + 1) * HT)
            prs = slice(2 * g, 2 * g + 2)
            for a, factor in ((0, lt[b]), (1, mb[b])):
                nc.vector.tensor_tensor(
                    out=pq[ht][:, a, g, :].rearrange("p (h s e) -> p h s e", s=2, e=2),
                    in0=bank, in1=factor[:, prs, cols, :].rearrange("p s h e -> p h s e"), op=ALU.mult,
                )

        def dhcopy(u):
            dhs[u] = prod.tile([P, HT * PACK], BANK_DT, name="dhs", tag="dhs", bufs=2)
            nc.scalar.copy(
                out=dhs[u][:].rearrange("p (h t) -> p h t", t=PACK),
                in_=dh[u][:].rearrange("p t h -> p h t"),
            )

        def gp_pmul(u):
            ht, g = divmod(u, G)
            b, hl = divmod(ht, HB // HT)
            bank = dhs[u][:].rearrange("p (h s e) -> p h s e", s=2, e=2)
            cols = slice(hl * HT, (hl + 1) * HT)
            prs = slice(2 * g, 2 * g + 2)
            for a, factor in ((1, mb[b]), (0, lt[b])):
                nc.gpsimd.tensor_tensor(
                    out=pq[ht][:, a, g, :].rearrange("p (h s e) -> p h s e", s=2, e=2),
                    in0=bank, in1=factor[:, prs, cols, :].rearrange("p s h e -> p h s e"), op=ALU.mult,
                )

        pc, ps = {}, {}

        def pquant(ht):
            pc[ht] = prod.tile([P, 2 * G * HT], U32, name="pc", tag="pc", align_bytes=64)
            ps[ht] = prod.tile([P, 2 * G * HT], U8, name="ps", tag="ps", align_bytes=64)
            nc.vector.quantize_mx(
                out=pc[ht][:].bitcast(FP8X4), scales=ps[ht][:],
                in_=pq[ht][:].rearrange("p a g c -> p (a g c)"),
            )

        acc = {}

        def stage2(ht):
            for a in range(2):
                acc[ht, a] = psum.tile([P, D], F32, name="acc", tag="acc")
                for g in range(G):
                    lo = (a * G + g) * HT
                    nc.tensor.matmul_mx(
                        out=acc[ht, a][:],
                        lhsT=pc[ht][:, lo:lo + HT].bitcast(FP8X4),
                        lhsT_scale=ps[ht][:, lo:lo + HT],
                        rhs=x_codes[:, g * D:(g + 1) * D].bitcast(FP8X4),
                        rhs_scale=x_scales[:, g * D:(g + 1) * D],
                        start=(g == 0), stop=(g == G - 1),
                    )

        def evac(engine, ht, a):
            res = stage.tile([P, D], F32, name="res", tag="res")
            if engine == "v":
                nc.vector.tensor_scalar(out=res[:], in0=acc[ht, a][:], scalar1=sgs[:, 0:1], scalar2=None, op0=ALU.mult)
            else:
                nc.scalar.activation(out=res[:], in_=acc[ht, a][:], func=ACT.Copy, scale=sgs[:, 0:1])
            nc.sync.dma_start(out=outs[a][ht * HT:(ht + 1) * HT, :], in_=res[:])

        ctx.enter_context(tc.manual_schedule(engines={ENG.Activation, ENG.DVE, ENG.Pool}))

        act_sig(0)
        act_sig(1)
        gw0 = interleave("v", w_raw[0][:])

        e_grp = {}
        for g in range(G):
            words = e_raw[g][:].bitcast(F32)
            e_grp[g] = grp.tile([P, HL * PACK], BF16, name="e_grouped", tag="grouped", align_bytes=64)
            egw = e_grp[g][:].bitcast(F32).rearrange("p (t m u) -> p t m u", t=PACK, u=2)
            for half in range(2):
                xt = psum.tile([P, PACK, P], F32, name="xt", tag="dh")
                for tt in range(2):
                    t = 2 * half + tt
                    for u in range(2):
                        nc.tensor.transpose(
                            out=xt[:, 2 * tt + u, :],
                            in_=words[:, t * 256 + u:(t + 1) * 256:2],
                            identity=ident[:],
                        )
                nc.scalar.copy(
                    out=egw[:, 2 * half:2 * half + 2, :, :],
                    in_=xt[:].rearrange("p (tt u) m -> p tt m u", u=2),
                )
        quantize(gw0, w_codes, w_scales, 0)
        gram = psum.tile([P, P], F32, name="gram", tag="acc")
        n_mm = G * PACK * (D // P)
        i_mm = 0
        for g in range(G):
            for t in range(PACK):
                for fb in range(D // P):
                    blk = e_raw[g][:, t * D + fb * P:t * D + (fb + 1) * P]
                    nc.tensor.matmul(out=gram[:], lhsT=blk, rhs=blk, start=(i_mm == 0), stop=(i_mm == n_mm - 1))
                    i_mm += 1
        act_sig(2)
        act_sig(3)
        for g in range(G):
            quantize(e_grp[g], e_codes, e_scales, g * K_PASS)
        nc.vector.scalar_tensor_tensor(
            out=diag[:], in0=gram[:], scalar=1.0, in1=ident[:], op0=ALU.mult, op1=ALU.mult,
            accum_out=ssq[:, 0:1],
        )
        tot = psum.tile([P, 2], F32, name="tot", tag="acc")
        nc.tensor.matmul(out=tot[:], lhsT=ones[:], rhs=ssq[:], start=True, stop=True)

        x_raw[0] = load_rows(x_pred, 0)
        x_raw[1] = load_rows(x_pred, 1)
        load_act(up_sb, up_pre, 1)
        load_act(gate_sb, gate_pre, 2)
        load_act(up_sb, up_pre, 2)
        w_raw[2] = load_w(2)
        load_act(gate_sb, gate_pre, 3)
        load_act(up_sb, up_pre, 3)
        w_raw[3] = load_w(3)

        xmul(0)
        xmul(1)
        nc.scalar.activation(out=em[:], in_=tot[:, 0:1], func=ACT.Sqrt, scale=1.0 / (N_TOK * N_TOK))
        nc.gpsimd.tensor_scalar(out=ema[:], in0=em[:], scalar1=0.05, scalar2=0.95, op0=ALU.mult, op1=ALU.add)
        nc.gpsimd.tensor_scalar(out=emc[:], in0=ema[:], scalar1=1e-8, scalar2=None, op0=ALU.max)
        act_m(0)
        act_l(0)
        stage1(3)
        dhcopy(3)
        gw1 = interleave("v", w_raw[1][:])
        nc.vector.reciprocal(out=rec[:], in_=emc[:])
        quantize(gw1, w_codes, w_scales, HL)
        nc.gpsimd.tensor_scalar(out=sgv[:], in0=rec[:], scalar1=em[:, 0:1], scalar2=3.0, op0=ALU.mult, op1=ALU.min)
        nc.gpsimd.tensor_scalar(out=sgs[:], in0=sgv[:], scalar1=1.0 / N_TOK, scalar2=None, op0=ALU.mult)
        gx0 = interleave("v", x_raw[0][:].rearrange("p (j d) -> p j d", j=PACK))
        gx1 = interleave("v", x_raw[1][:].rearrange("p (j d) -> p j d", j=PACK))
        quantize(gx0, x_codes, x_scales, 0)
        quantize(gx1, x_codes, x_scales, D)
        act_m(1)
        act_l(1)
        bmul(0)

        gw_late = {}
        for u in range(3):
            stage1(u)
        for b in range(N_HB):
            u0 = 4 * b
            ht0, ht1 = 2 * b, 2 * b + 1
            more = b + 1 < N_HB
            new_pq(ht0)
            new_pq(ht1)
            gp_pmul(u0 + 3)
            if b < 4:
                c_late, half = 2 + b // 2, b % 2
                if half == 0:
                    gw_late[c_late] = grp.tile([P, HL * PACK], BF16, name="grouped", tag="grouped", align_bytes=64)
                interleave_half(gw_late[c_late], w_raw[c_late], half)
            if more:
                stage1(u0 + 7)
                dhcopy(u0 + 7)
            if b >= 1:
                evac("s", ht0 - 1, 0)
                evac("s", ht0 - 1, 1)
            if b == 3:
                act_sig(7)
            if b + 2 < N_HB:
                act_m(b + 2)
                act_l(b + 2)
            if b == 2:
                act_sig(4)
            for i in range(3):
                pmul(u0 + i)
                if more:
                    stage1(u0 + 4 + i)
            pquant(ht0)
            stage2(ht0)
            if b < 2:
                xmul(b + 2)
            if 4 <= b + 1 < N_HB:
                xmul(b + 1)
            if b in (2, 4):
                quantize(gw_late[1 + b // 2], w_codes, w_scales, (1 + b // 2) * HL)
            pquant(ht1)
            stage2(ht1)
            if more:
                bmul(b + 1)
            evac("s", ht0, 0)
            evac("s", ht0, 1)
            if b == 2:
                act_sig(5)
                act_sig(6)
        evac("s", N_HT - 1, 0)
        evac("v", N_HT - 1, 1)
